import numpy as np
import ml_dtypes


def mxq(x, axis, fmt="e4m3"):
    dtype, down = {"e4m3": (ml_dtypes.float8_e4m3fn, 7), "e5m2": (ml_dtypes.float8_e5m2, 14)}[fmt]
    v = np.moveaxis(np.asarray(x, np.float32).astype(ml_dtypes.bfloat16).astype(np.float64), axis, -1)
    blocks = v.reshape(v.shape[:-1] + (-1, 32))
    amax = np.abs(blocks).max(-1, keepdims=True)
    byte = np.maximum(np.where(amax > 0, np.frexp(amax)[1] - 1 + 127, 0) - down, 1)
    scale = np.exp2(byte - 127.0)
    codes = (blocks / scale).astype(np.float32).astype(dtype).astype(np.float64)
    return np.moveaxis((codes * scale).reshape(v.shape), -1, axis)


WIDE = False


def mx_kscale(k):
    if not WIDE:
        return np.ones(k)
    levels = np.array([10, -10, 5, -5, 0])
    a = np.random.permutation(np.resize(levels, k // 512 * 4)).reshape(k // 512, 4)
    idx = np.arange(k)
    return np.exp2(a[idx // 512, idx % 128 // 32])


BF16 = ml_dtypes.bfloat16


def bf(x):
    return np.asarray(x, np.float32).astype(BF16)


def f64(x):
    return np.asarray(x).astype(np.float64)


B, S, D, C = 8, 512, 256, 512


def setup_inputs():
    s = mx_kscale(S)
    a = D ** -0.25
    return {"q_rot": bf(np.random.standard_normal((B, S, D)) * a),
            "k_rot": bf(np.random.standard_normal((B, S, D)) * a * s[:, None]),
            "v": bf(np.random.standard_normal((B, S, D)) * 0.5 / s[:, None]),
            "gamma": bf(1.0 - 0.00390625 * np.random.randint(1, 3, (1,)))}


def reference(q_rot, k_rot, v, gamma):
    q, k, g = f64(q_rot), f64(k_rot), f64(gamma)[0]
    vq = mxq(f64(v), 1, "e4m3")
    pos = np.arange(S)
    out = []
    for i in range(S // C):
        lo, hi = i * C, (i + 1) * C
        diff = pos[lo:hi, None] - pos[None, :hi]
        causal = diff >= 0
        decay = np.where(causal, g ** np.where(causal, diff, 0), 0.0)
        scores = q[:, lo:hi] @ k[:, :hi].transpose(0, 2, 1)
        p = scores * decay[None]
        out.append(mxq(p, 2, "e4m3") @ vq[:, :hi])
    return np.concatenate(out, axis=1)

@@ -1,0 +1,162 @@
+from contextlib import ExitStack
+
+import concourse.mybir as mybir
+from concourse.masks import make_identity
+
+F32 = mybir.dt.float32
+BF16 = mybir.dt.bfloat16
+U32 = mybir.dt.uint32
+U8 = mybir.dt.uint8
+FP8X4 = mybir.dt.float8_e4m3fn_x4
+MULT = mybir.AluOpType.mult
+ADD = mybir.AluOpType.add
+
+B, S, D = 8, 512, 256
+P = 128
+NCH = S // P
+FLOPS = 4 * B * S * S * D
+DV = 96
+
+
+def tile_retention_pa_kernel(tc, q_rot, k_rot, v, gamma, out):
+    nc = tc.nc
+    with ExitStack() as ctx:
+        const = ctx.enter_context(tc.tile_pool(name="const", bufs=1))
+        inp = ctx.enter_context(tc.tile_pool(name="inp", bufs=1))
+        work = ctx.enter_context(tc.tile_pool(name="work", bufs=3))
+        ps_t = ctx.enter_context(tc.psum_pool(name="ps_t", bufs=2))
+        ps_s = ctx.enter_context(tc.psum_pool(name="ps_s", bufs=4))
+        ps_o = ctx.enter_context(tc.psum_pool(name="ps_o", bufs=2))
+        ctx.enter_context(tc.manual_schedule())
+
+        gam_bf = const.tile([P, 1], BF16, name="gam_bf")
+        nc.scalar.dma_start(out=gam_bf[:], in_=gamma.partition_broadcast(P))
+        q_sb, k_sb, v_sb = [], [], []
+        for b in range(B):
+            qt = inp.tile([P, NCH, D], BF16, name="q_sb%d" % b)
+            nc.sync.dma_start(out=qt[:], in_=q_rot[b].rearrange("(p j) d -> p j d", j=NCH))
+            kt = inp.tile([P, NCH, D], BF16, name="k_sb%d" % b)
+            nc.sync.dma_start(out=kt[:], in_=k_rot[b].rearrange("(p j) d -> p j d", j=NCH))
+            vt = inp.tile([P, NCH, D], BF16, name="v_sb%d" % b)
+            nc.sync.dma_start(out=vt[:], in_=v[b].rearrange("(t p) d -> p t d", p=P))
+            q_sb.append(qt)
+            k_sb.append(kt)
+            v_sb.append(vt)
+
+        idz = const.tile([P, S], F32, name="idz")
+        nc.gpsimd.memset(idz[:], 0.0)
+        make_identity(nc, idz[:, 0:P])
+        ident = idz[:, 0:P]
+        grouped = []
+        for i in range(3):
+            g = const.tile([P, NCH, P, NCH], BF16, name="grouped%d" % i, align_bytes=64)
+            nc.vector.memset(g[:], 0.0)
+            grouped.append(g)
+        gam = const.tile([P, 1], F32, name="gam")
+        nc.vector.tensor_copy(out=gam[:], in_=gam_bf[:])
+        w = const.tile([P, S], F32, name="w")
+        nc.vector.tensor_tensor_scan(
+            out=w[:], data0=gam[:, 0:1].to_broadcast([P, S]), data1=idz[:],
+            initial=0.0, op0=MULT, op1=ADD,
+        )
+        dec = const.tile([P, P, NCH], F32, name="dec")
+        for s in range(NCH):
+            nc.vector.tensor_copy(out=dec[:, :, s], in_=w[:, (NCH - 1 - s) * P : (NCH - s) * P])
+
+        qT, kT, vgs, vcs, vss, pcs, pss = {}, {}, {}, {}, {}, {}, {}
+
+        def transposes(b):
+            for src, dst, nm in ((k_sb[b], kT, "kT"), (q_sb[b], qT, "qT")):
+                tp = ps_t.tile([P, NCH, P], F32, name="tp")
+                for j in range(NCH):
+                    nc.tensor.transpose(tp[:, j, :], src[:, j, :].bitcast(F32), ident)
+                t = work.tile([P, P, NCH], F32, name=nm)
+                nc.scalar.copy(out=t[:], in_=tp[:].rearrange("w j p -> w p j"))
+                dst[b] = t[:].rearrange("w p j -> w (p j)").bitcast(BF16).rearrange("w (n e) -> w n e", e=2)
+
+        def scores_and_decay(b):
+            g = grouped[b % 3]
+            for c in range(NCH):
+                sc = ps_s.tile([P, NCH, P], F32, name="sc")
+                for j in range(c + 1):
+                    for e in range(2):
+                        nc.tensor.matmul(
+                            sc[:, j, :],
+                            lhsT=kT[b][:, j * P : (j + 1) * P, e],
+                            rhs=qT[b][:, c * P : (c + 1) * P, e],
+                            start=(e == 0), stop=(e == 1),
+                        )
+                nc.vector.tensor_tensor(
+                    out=g[:, c, :, 0 : c + 1],
+                    in0=sc[:, 0 : c + 1, :].rearrange("p j r -> p r j"),
+                    in1=dec[:, :, NCH - 1 - c : NCH],
+                    op=MULT,
+                )
+
+        def regroup_v(b):
+            vg = work.tile([P, D, NCH], BF16, name="vg", align_bytes=64)
+            nc.vector.tensor_copy(
+                out=vg[:, 0:DV, :].rearrange("p (c i) t -> p c t i", i=4),
+                in_=v_sb[b][:, :, 0:DV].rearrange("p t (c i) -> p c t i", i=4),
+            )
+            nc.scalar.copy(
+                out=vg[:, DV:D, :].rearrange("p (c i) t -> p c t i", i=4),
+                in_=v_sb[b][:, :, DV:D].rearrange("p t (c i) -> p c t i", i=4),
+            )
+            vgs[b] = vg
+
+        def quantise_v(b):
+            vc = work.tile([P, D], U32, name="vc", align_bytes=64)
+            vs = work.tile([P, D], U8, name="vs", align_bytes=64)
+            nc.vector.quantize_mx(
+                out=vc[:].bitcast(FP8X4), scales=vs[:],
+                in_=vgs[b][:].rearrange("p d t -> p (d t)"),
+            )
+            vcs[b], vss[b] = vc, vs
+
+        def quantise_p(b):
+            pc = work.tile([P, S], U32, name="pc", align_bytes=64)
+            ps = work.tile([P, S], U8, name="ps", align_bytes=64)
+            nc.vector.quantize_mx(
+                out=pc[:].bitcast(FP8X4), scales=ps[:],
+                in_=grouped[b % 3][:].rearrange("p c r j -> p (c r j)"),
+            )
+            pcs[b], pss[b] = pc, ps
+
+        def second_matmul(b):
+            for h in range(2):
+                o = ps_o.tile([P, 2, D], F32, name="o")
+                for i in range(2):
+                    c = 2 * h + i
+                    nc.tensor.matmul_mx(
+                        o[:, i, :],
+                        lhsT=pcs[b][:, c * P : (c + 1) * P].bitcast(FP8X4),
+                        lhsT_scale=pss[b][:, c * P : (c + 1) * P],
+                        rhs=vcs[b][:].bitcast(FP8X4),
+                        rhs_scale=vss[b][:],
+                        start=True, stop=True,
+                    )
+                ot = work.tile([P, 2, D], F32, name="ot")
+                nc.scalar.copy(out=ot[:], in_=o[:])
+                nc.sync.dma_start(
+                    out=out[b, 2 * h * P : (2 * h + 2) * P, :].rearrange("(c r) d -> r c d", r=P),
+                    in_=ot[:],
+                )
+
+        transposes(0)
+        regroup_v(0)
+        for k in range(B + 1):
+            if k < B:
+                scores_and_decay(k)
+            if k == 0:
+                transposes(1)
+            if k + 2 < B:
+                transposes(k + 2)
+            if k < B:
+                quantise_v(k)
+            if k + 1 < B:
+                regroup_v(k + 1)
+            if k < B:
+                quantise_p(k)
+            if k >= 1:
+                second_matmul(k - 1)

@@ -15,7 +15,6 @@ B, S, D = 8, 512, 256
 P = 128
 NCH = S // P
 FLOPS = 4 * B * S * S * D
-DV = 96
 
 
 def tile_retention_pa_kernel(tc, q_rot, k_rot, v, gamma, out):
@@ -24,19 +23,18 @@ def tile_retention_pa_kernel(tc, q_rot, k_rot, v, gamma, out):
         const = ctx.enter_context(tc.tile_pool(name="const", bufs=1))
         inp = ctx.enter_context(tc.tile_pool(name="inp", bufs=1))
         work = ctx.enter_context(tc.tile_pool(name="work", bufs=3))
-        ps_t = ctx.enter_context(tc.psum_pool(name="ps_t", bufs=2))
-        ps_s = ctx.enter_context(tc.psum_pool(name="ps_s", bufs=4))
-        ps_o = ctx.enter_context(tc.psum_pool(name="ps_o", bufs=2))
+        outp = ctx.enter_context(tc.tile_pool(name="outp", bufs=4))
+        psum = ctx.enter_context(tc.psum_pool(name="psum", bufs=1))
         ctx.enter_context(tc.manual_schedule())
 
         gam_bf = const.tile([P, 1], BF16, name="gam_bf")
         nc.scalar.dma_start(out=gam_bf[:], in_=gamma.partition_broadcast(P))
         q_sb, k_sb, v_sb = [], [], []
         for b in range(B):
-            qt = inp.tile([P, NCH, D], BF16, name="q_sb%d" % b)
-            nc.sync.dma_start(out=qt[:], in_=q_rot[b].rearrange("(p j) d -> p j d", j=NCH))
             kt = inp.tile([P, NCH, D], BF16, name="k_sb%d" % b)
             nc.sync.dma_start(out=kt[:], in_=k_rot[b].rearrange("(p j) d -> p j d", j=NCH))
+            qt = inp.tile([P, NCH, D], BF16, name="q_sb%d" % b)
+            nc.sync.dma_start(out=qt[:], in_=q_rot[b].rearrange("(p j) d -> p j d", j=NCH))
             vt = inp.tile([P, NCH, D], BF16, name="v_sb%d" % b)
             nc.sync.dma_start(out=vt[:], in_=v[b].rearrange("(t p) d -> p t d", p=P))
             q_sb.append(qt)
@@ -63,49 +61,66 @@ def tile_retention_pa_kernel(tc, q_rot, k_rot, v, gamma, out):
         for s in range(NCH):
             nc.vector.tensor_copy(out=dec[:, :, s], in_=w[:, (NCH - 1 - s) * P : (NCH - s) * P])
 
-        qT, kT, vgs, vcs, vss, pcs, pss = {}, {}, {}, {}, {}, {}, {}
+        qT, kT, scs, vgs, vcs, vss, pcs, pss = {}, {}, {}, {}, {}, {}, {}, {}
 
-        def transposes(b):
-            for src, dst, nm in ((k_sb[b], kT, "kT"), (q_sb[b], qT, "qT")):
-                tp = ps_t.tile([P, NCH, P], F32, name="tp")
-                for j in range(NCH):
-                    nc.tensor.transpose(tp[:, j, :], src[:, j, :].bitcast(F32), ident)
-                t = work.tile([P, P, NCH], F32, name=nm)
-                nc.scalar.copy(out=t[:], in_=tp[:].rearrange("w j p -> w p j"))
-                dst[b] = t[:].rearrange("w p j -> w (p j)").bitcast(BF16).rearrange("w (n e) -> w n e", e=2)
+        def ok(b):
+            return 0 <= b < B
 
-        def scores_and_decay(b):
-            g = grouped[b % 3]
-            for c in range(NCH):
-                sc = ps_s.tile([P, NCH, P], F32, name="sc")
-                for j in range(c + 1):
-                    for e in range(2):
-                        nc.tensor.matmul(
-                            sc[:, j, :],
-                            lhsT=kT[b][:, j * P : (j + 1) * P, e],
-                            rhs=qT[b][:, c * P : (c + 1) * P, e],
-                            start=(e == 0), stop=(e == 1),
-                        )
-                nc.vector.tensor_tensor(
-                    out=g[:, c, :, 0 : c + 1],
-                    in0=sc[:, 0 : c + 1, :].rearrange("p j r -> p r j"),
-                    in1=dec[:, :, NCH - 1 - c : NCH],
-                    op=MULT,
-                )
+        def transpose(b, src, dst, nm):
+            if not ok(b):
+                return
+            tp = psum.tile([P, NCH, P], F32, name="tp_" + nm)
+            for j in range(NCH):
+                nc.tensor.transpose(tp[:, j, :], src[b][:, j, :].bitcast(F32), ident)
+            t = work.tile([P, P, NCH], F32, name=nm)
+            nc.scalar.copy(out=t[:], in_=tp[:].rearrange("w j p -> w p j"))
+            dst[b] = t[:].rearrange("w p j -> w (p j)").bitcast(BF16).rearrange("w (n e) -> w n e", e=2)
+
+        def scores(b, c):
+            if not ok(b):
+                return
+            sc = psum.tile([P, c + 1, P], F32, name="sc%d" % c)
+            for j in range(c + 1):
+                for e in range(2):
+                    nc.tensor.matmul(
+                        sc[:, j, :],
+                        lhsT=kT[b][:, j * P : (j + 1) * P, e],
+                        rhs=qT[b][:, c * P : (c + 1) * P, e],
+                        start=(e == 0), stop=(e == 1),
+                    )
+            scs[(b, c)] = sc
+
+        def decay(b, c):
+            if not ok(b):
+                return
+            nc.vector.tensor_tensor(
+                out=grouped[b % 3][:, c, :, 0 : c + 1],
+                in0=scs[(b, c)][:].rearrange("p j r -> p r j"),
+                in1=dec[:, :, NCH - 1 - c : NCH],
+                op=MULT,
+            )
+
+        def chunk0(b):
+            if not ok(b):
+                return
+            scores(b, 0)
+            s0 = work.tile([P, P], F32, name="s0")
+            nc.scalar.copy(out=s0[:], in_=scs[(b, 0)][:, 0, :])
+            nc.gpsimd.tensor_tensor(out=grouped[b % 3][:, 0, :, 0], in0=s0[:], in1=w[:, 0:P], op=MULT)
 
         def regroup_v(b):
+            if not ok(b):
+                return
             vg = work.tile([P, D, NCH], BF16, name="vg", align_bytes=64)
             nc.vector.tensor_copy(
-                out=vg[:, 0:DV, :].rearrange("p (c i) t -> p c t i", i=4),
-                in_=v_sb[b][:, :, 0:DV].rearrange("p t (c i) -> p c t i", i=4),
-            )
-            nc.scalar.copy(
-                out=vg[:, DV:D, :].rearrange("p (c i) t -> p c t i", i=4),
-                in_=v_sb[b][:, :, DV:D].rearrange("p t (c i) -> p c t i", i=4),
+                out=vg[:].rearrange("p (c i) t -> p c t i", i=4),
+                in_=v_sb[b][:].rearrange("p t (c i) -> p c t i", i=4),
             )
             vgs[b] = vg
 
         def quantise_v(b):
+            if not ok(b):
+                return
             vc = work.tile([P, D], U32, name="vc", align_bytes=64)
             vs = work.tile([P, D], U8, name="vs", align_bytes=64)
             nc.vector.quantize_mx(
@@ -115,6 +130,8 @@ def tile_retention_pa_kernel(tc, q_rot, k_rot, v, gamma, out):
             vcs[b], vss[b] = vc, vs
 
         def quantise_p(b):
+            if not ok(b):
+                return
             pc = work.tile([P, S], U32, name="pc", align_bytes=64)
             ps = work.tile([P, S], U8, name="ps", align_bytes=64)
             nc.vector.quantize_mx(
@@ -124,8 +141,10 @@ def tile_retention_pa_kernel(tc, q_rot, k_rot, v, gamma, out):
             pcs[b], pss[b] = pc, ps
 
         def second_matmul(b):
+            if not ok(b):
+                return
             for h in range(2):
-                o = ps_o.tile([P, 2, D], F32, name="o")
+                o = psum.tile([P, 2, D], F32, name="o%d" % h)
                 for i in range(2):
                     c = 2 * h + i
                     nc.tensor.matmul_mx(
@@ -136,27 +155,27 @@ def tile_retention_pa_kernel(tc, q_rot, k_rot, v, gamma, out):
                         rhs_scale=vss[b][:],
                         start=True, stop=True,
                     )
-                ot = work.tile([P, 2, D], F32, name="ot")
+                ot = outp.tile([P, 2, D], F32, name="ot")
                 nc.scalar.copy(out=ot[:], in_=o[:])
                 nc.sync.dma_start(
                     out=out[b, 2 * h * P : (2 * h + 2) * P, :].rearrange("(c r) d -> r c d", r=P),
                     in_=ot[:],
                 )
 
-        transposes(0)
-        regroup_v(0)
-        for k in range(B + 1):
-            if k < B:
-                scores_and_decay(k)
-            if k == 0:
-                transposes(1)
-            if k + 2 < B:
-                transposes(k + 2)
-            if k < B:
-                quantise_v(k)
-            if k + 1 < B:
-                regroup_v(k + 1)
-            if k < B:
-                quantise_p(k)
-            if k >= 1:
-                second_matmul(k - 1)
+        transpose(0, k_sb, kT, "kT")
+        transpose(0, q_sb, qT, "qT")
+        chunk0(0)
+        for k in range(-1, B + 1):
+            second_matmul(k - 1)
+            decay(k, 1)
+            scores(k + 1, 1)
+            transpose(k + 2, k_sb, kT, "kT")
+            decay(k, 2)
+            scores(k + 1, 2)
+            transpose(k + 2, q_sb, qT, "qT")
+            decay(k, 3)
+            scores(k + 1, 3)
+            chunk0(k + 2)
+            regroup_v(k + 1)
+            quantise_p(k)
+            quantise_v(k + 1)

@@ -15,6 +15,7 @@ B, S, D = 8, 512, 256
 P = 128
 NCH = S // P
 FLOPS = 4 * B * S * S * D
+NG = 2
 
 
 def tile_retention_pa_kernel(tc, q_rot, k_rot, v, gamma, out):
@@ -22,31 +23,41 @@ def tile_retention_pa_kernel(tc, q_rot, k_rot, v, gamma, out):
     with ExitStack() as ctx:
         const = ctx.enter_context(tc.tile_pool(name="const", bufs=1))
         inp = ctx.enter_context(tc.tile_pool(name="inp", bufs=1))
-        work = ctx.enter_context(tc.tile_pool(name="work", bufs=3))
-        outp = ctx.enter_context(tc.tile_pool(name="outp", bufs=4))
+        work2 = ctx.enter_context(tc.tile_pool(name="work2", bufs=2))
+        work3 = ctx.enter_context(tc.tile_pool(name="work3", bufs=3))
+        work4 = ctx.enter_context(tc.tile_pool(name="work4", bufs=4))
         psum = ctx.enter_context(tc.psum_pool(name="psum", bufs=1))
         ctx.enter_context(tc.manual_schedule())
 
         gam_bf = const.tile([P, 1], BF16, name="gam_bf")
         nc.scalar.dma_start(out=gam_bf[:], in_=gamma.partition_broadcast(P))
-        q_sb, k_sb, v_sb = [], [], []
-        for b in range(B):
-            kt = inp.tile([P, NCH, D], BF16, name="k_sb%d" % b)
-            nc.sync.dma_start(out=kt[:], in_=k_rot[b].rearrange("(p j) d -> p j d", j=NCH))
-            qt = inp.tile([P, NCH, D], BF16, name="q_sb%d" % b)
-            nc.sync.dma_start(out=qt[:], in_=q_rot[b].rearrange("(p j) d -> p j d", j=NCH))
-            vt = inp.tile([P, NCH, D], BF16, name="v_sb%d" % b)
-            nc.sync.dma_start(out=vt[:], in_=v[b].rearrange("(t p) d -> p t d", p=P))
-            q_sb.append(qt)
-            k_sb.append(kt)
-            v_sb.append(vt)
+        q_sb, k_sb, v_sb = {}, {}, {}
+
+        def load(kind, b):
+            t = inp.tile([P, NCH, D], BF16, name="%s_sb%d" % (kind, b))
+            if kind == "k":
+                nc.sync.dma_start(out=t[:], in_=k_rot[b].rearrange("(p j) d -> p j d", j=NCH))
+                k_sb[b] = t
+            elif kind == "q":
+                nc.sync.dma_start(out=t[:], in_=q_rot[b].rearrange("(p j) d -> p j d", j=NCH))
+                q_sb[b] = t
+            else:
+                nc.sync.dma_start(out=t[:], in_=v[b].rearrange("(t p) d -> p t d", p=P))
+                v_sb[b] = t
+
+        for kind, b in (("k", 0), ("q", 0), ("v", 0), ("v", 1), ("k", 1), ("q", 1)):
+            load(kind, b)
+        for b in range(2, B):
+            load("k", b)
+            load("q", b)
+            load("v", b)
 
         idz = const.tile([P, S], F32, name="idz")
         nc.gpsimd.memset(idz[:], 0.0)
         make_identity(nc, idz[:, 0:P])
         ident = idz[:, 0:P]
         grouped = []
-        for i in range(3):
+        for i in range(NG):
             g = const.tile([P, NCH, P, NCH], BF16, name="grouped%d" % i, align_bytes=64)
             nc.vector.memset(g[:], 0.0)
             grouped.append(g)
@@ -61,57 +72,76 @@ def tile_retention_pa_kernel(tc, q_rot, k_rot, v, gamma, out):
         for s in range(NCH):
             nc.vector.tensor_copy(out=dec[:, :, s], in_=w[:, (NCH - 1 - s) * P : (NCH - s) * P])
 
-        qT, kT, scs, vgs, vcs, vss, pcs, pss = {}, {}, {}, {}, {}, {}, {}, {}
+        qT, kT, scs, s01s, vgs, vcs, vss, pcs, pss = {}, {}, {}, {}, {}, {}, {}, {}, {}
 
         def ok(b):
             return 0 <= b < B
 
-        def transpose(b, src, dst, nm):
+        def transpose(b, kind):
             if not ok(b):
                 return
-            tp = psum.tile([P, NCH, P], F32, name="tp_" + nm)
+            src, dst = (k_sb, kT) if kind == "k" else (q_sb, qT)
+            tp = psum.tile([P, NCH, P], F32, name="tp_" + kind)
             for j in range(NCH):
                 nc.tensor.transpose(tp[:, j, :], src[b][:, j, :].bitcast(F32), ident)
-            t = work.tile([P, P, NCH], F32, name=nm)
+            t = work4.tile([P, P, NCH], F32, name=kind + "T")
             nc.scalar.copy(out=t[:], in_=tp[:].rearrange("w j p -> w p j"))
             dst[b] = t[:].rearrange("w p j -> w (p j)").bitcast(BF16).rearrange("w (n e) -> w n e", e=2)
+
+        def score_tile(b, dst, j, c):
+            for e in range(2):
+                nc.tensor.matmul(
+                    dst,
+                    lhsT=kT[b][:, j * P : (j + 1) * P, e],
+                    rhs=qT[b][:, c * P : (c + 1) * P, e],
+                    start=(e == 0), stop=(e == 1),
+                )
 
         def scores(b, c):
             if not ok(b):
                 return
             sc = psum.tile([P, c + 1, P], F32, name="sc%d" % c)
             for j in range(c + 1):
-                for e in range(2):
-                    nc.tensor.matmul(
-                        sc[:, j, :],
-                        lhsT=kT[b][:, j * P : (j + 1) * P, e],
-                        rhs=qT[b][:, c * P : (c + 1) * P, e],
-                        start=(e == 0), stop=(e == 1),
-                    )
+                score_tile(b, sc[:, j, :], j, c)
             scs[(b, c)] = sc
 
         def decay(b, c):
             if not ok(b):
                 return
             nc.vector.tensor_tensor(
-                out=grouped[b % 3][:, c, :, 0 : c + 1],
+                out=grouped[b % NG][:, c, :, 0 : c + 1],
                 in0=scs[(b, c)][:].rearrange("p j r -> p r j"),
                 in1=dec[:, :, NCH - 1 - c : NCH],
                 op=MULT,
             )
 
-        def chunk0(b):
+        def scores01(b):
             if not ok(b):
                 return
-            scores(b, 0)
-            s0 = work.tile([P, P], F32, name="s0")
-            nc.scalar.copy(out=s0[:], in_=scs[(b, 0)][:, 0, :])
-            nc.gpsimd.tensor_tensor(out=grouped[b % 3][:, 0, :, 0], in0=s0[:], in1=w[:, 0:P], op=MULT)
+            sc = psum.tile([P, 3, P], F32, name="sc01")
+            score_tile(b, sc[:, 0, :], 0, 0)
+            score_tile(b, sc[:, 1, :], 0, 1)
+            score_tile(b, sc[:, 2, :], 1, 1)
+            s01 = work2.tile([P, 3, P], F32, name="s01")
+            nc.scalar.copy(out=s01[:], in_=sc[:])
+            s01s[b] = s01
+
+        def decay01(b):
+            if not ok(b):
+                return
+            g = grouped[b % NG]
+            nc.gpsimd.tensor_tensor(out=g[:, 0, :, 0], in0=s01s[b][:, 0, :], in1=w[:, 0:P], op=MULT)
+            nc.gpsimd.tensor_tensor(
+                out=g[:, 1, :, 0:2],
+                in0=s01s[b][:, 1:3, :].rearrange("p j r -> p r j"),
+                in1=dec[:, :, 2:4],
+                op=MULT,
+            )
 
         def regroup_v(b):
             if not ok(b):
                 return
-            vg = work.tile([P, D, NCH], BF16, name="vg", align_bytes=64)
+            vg = work3.tile([P, D, NCH], BF16, name="vg", align_bytes=64)
             nc.vector.tensor_copy(
                 out=vg[:].rearrange("p (c i) t -> p c t i", i=4),
                 in_=v_sb[b][:].rearrange("p t (c i) -> p c t i", i=4),
@@ -121,61 +151,91 @@ def tile_retention_pa_kernel(tc, q_rot, k_rot, v, gamma, out):
         def quantise_v(b):
             if not ok(b):
                 return
-            vc = work.tile([P, D], U32, name="vc", align_bytes=64)
-            vs = work.tile([P, D], U8, name="vs", align_bytes=64)
+            vc = work3.tile([P, D], U32, name="vc", align_bytes=64)
+            vs = work3.tile([P, D], U8, name="vs", align_bytes=64)
             nc.vector.quantize_mx(
                 out=vc[:].bitcast(FP8X4), scales=vs[:],
                 in_=vgs[b][:].rearrange("p d t -> p (d t)"),
             )
             vcs[b], vss[b] = vc, vs
 
-        def quantise_p(b):
-            if not ok(b):
-                return
-            pc = work.tile([P, S], U32, name="pc", align_bytes=64)
-            ps = work.tile([P, S], U8, name="ps", align_bytes=64)
+        def quantise_p(b, c0, c1):
+            if c0 == 0:
+                pcs[b] = work3.tile([P, S], U32, name="pc", align_bytes=64)
+                pss[b] = work3.tile([P, S], U8, name="ps", align_bytes=64)
             nc.vector.quantize_mx(
-                out=pc[:].bitcast(FP8X4), scales=ps[:],
-                in_=grouped[b % 3][:].rearrange("p c r j -> p (c r j)"),
+                out=pcs[b][:, c0 * P : c1 * P].bitcast(FP8X4), scales=pss[b][:, c0 * P : c1 * P],
+                in_=grouped[b % NG][:, c0:c1].rearrange("p c r j -> p (c r j)"),
             )
-            pcs[b], pss[b] = pc, ps
 
-        def second_matmul(b):
-            if not ok(b):
-                return
-            for h in range(2):
-                o = psum.tile([P, 2, D], F32, name="o%d" % h)
-                for i in range(2):
-                    c = 2 * h + i
-                    nc.tensor.matmul_mx(
-                        o[:, i, :],
-                        lhsT=pcs[b][:, c * P : (c + 1) * P].bitcast(FP8X4),
-                        lhsT_scale=pss[b][:, c * P : (c + 1) * P],
-                        rhs=vcs[b][:].bitcast(FP8X4),
-                        rhs_scale=vss[b][:],
-                        start=True, stop=True,
-                    )
-                ot = outp.tile([P, 2, D], F32, name="ot")
-                nc.scalar.copy(out=ot[:], in_=o[:])
-                nc.sync.dma_start(
-                    out=out[b, 2 * h * P : (2 * h + 2) * P, :].rearrange("(c r) d -> r c d", r=P),
-                    in_=ot[:],
-                )
+        def mx_pass(b, c, dst):
+            nc.tensor.matmul_mx(
+                dst,
+                lhsT=pcs[b][:, c * P : (c + 1) * P].bitcast(FP8X4),
+                lhsT_scale=pss[b][:, c * P : (c + 1) * P],
+                rhs=vcs[b][:].bitcast(FP8X4),
+                rhs_scale=vss[b][:],
+                start=True, stop=True,
+            )
 
-        transpose(0, k_sb, kT, "kT")
-        transpose(0, q_sb, qT, "qT")
-        chunk0(0)
-        for k in range(-1, B + 1):
-            second_matmul(k - 1)
-            decay(k, 1)
-            scores(k + 1, 1)
-            transpose(k + 2, k_sb, kT, "kT")
+        def second_matmul_half(b, h):
+            o = psum.tile([P, 2, D], F32, name="o%d" % h)
+            for i in range(2):
+                mx_pass(b, 2 * h + i, o[:, i, :])
+            ot = work4.tile([P, 2, D], F32, name="ot")
+            nc.scalar.copy(out=ot[:], in_=o[:])
+            nc.sync.dma_start(
+                out=out[b, 2 * h * P : (2 * h + 2) * P, :].rearrange("(c r) d -> r c d", r=P),
+                in_=ot[:],
+            )
+
+        transpose(0, "k")
+        transpose(0, "q")
+        scores01(0)
+        decay01(0)
+        regroup_v(0)
+        for k in range(-1, B):
+            last = k == B - 1
+            if ok(k - 1):
+                second_matmul_half(k - 1, 0)
+                second_matmul_half(k - 1, 1)
+            if k == 0:
+                transpose(2, "k")
+                transpose(2, "q")
+            elif k > 0:
+                transpose(k + 3, "k")
             decay(k, 2)
+            if last:
+                quantise_p(k, 0, 2)
             scores(k + 1, 2)
-            transpose(k + 2, q_sb, qT, "qT")
+            if k == 0:
+                transpose(3, "k")
+                transpose(3, "q")
+            elif k > 0:
+                transpose(k + 3, "q")
             decay(k, 3)
             scores(k + 1, 3)
-            chunk0(k + 2)
-            regroup_v(k + 1)
-            quantise_p(k)
+            if k == -1:
+                transpose(1, "k")
+                transpose(1, "q")
+            scores01(k + 2)
+            regroup_v(k + 2)
             quantise_v(k + 1)
+            if last:
+                second_matmul_half(k, 0)
+                quantise_p(k, 2, 4)
+            elif ok(k):
+                quantise_p(k, 0, 4)
+            decay01(k + 2)
+
+        b = B - 1
+        o_a = psum.tile([P, D], F32, name="o1")
+        mx_pass(b, 2, o_a[:])
+        o_b = psum.tile([P, D], F32, name="o2")
+        mx_pass(b, 3, o_b[:])
+        ot_a = work4.tile([P, D], F32, name="ot_a")
+        nc.scalar.copy(out=ot_a[:], in_=o_a[:])
+        nc.scalar.dma_start(out=out[b, 2 * P : 3 * P, :], in_=ot_a[:])
+        ot_b = work4.tile([P, D], F32, name="ot_b")
+        nc.vector.tensor_copy(out=ot_b[:], in_=o_b[:])
+        nc.sync.dma_start(out=out[b, 3 * P : 4 * P, :], in_=ot_b[:])

@@ -34,23 +34,33 @@ def tile_retention_pa_kernel(tc, q_rot, k_rot, v, gamma, out):
         q_sb, k_sb, v_sb = {}, {}, {}
 
         def load(kind, b):
-            t = inp.tile([P, NCH, D], BF16, name="%s_sb%d" % (kind, b))
+            if kind == "v":
+                t2 = inp.tile([P, 2, NCH, D], BF16, name="v_sb%d" % b)
+                for t in range(NCH):
+                    j = NCH - 1 - t
+                    nc.sync.dma_start(
+                        out=t2[:, :, t, :],
+                        in_=v[b : b + 2, j * P : (j + 1) * P, :].rearrange("b p d -> p b d"),
+                    )
+                v_sb[b] = t2[:, 0]
+                v_sb[b + 1] = t2[:, 1]
+                return
+            t1 = inp.tile([P, NCH, D], BF16, name="%s_sb%d" % (kind, b))
             if kind == "k":
-                nc.sync.dma_start(out=t[:], in_=k_rot[b].rearrange("(p j) d -> p j d", j=NCH))
-                k_sb[b] = t
-            elif kind == "q":
-                nc.sync.dma_start(out=t[:], in_=q_rot[b].rearrange("(p j) d -> p j d", j=NCH))
-                q_sb[b] = t
+                nc.sync.dma_start(out=t1[:], in_=k_rot[b].rearrange("(p j) d -> p j d", j=NCH))
+                k_sb[b] = t1
             else:
-                nc.sync.dma_start(out=t[:], in_=v[b].rearrange("(t p) d -> p t d", p=P))
-                v_sb[b] = t
+                nc.sync.dma_start(out=t1[:], in_=q_rot[b].rearrange("(p j) d -> p j d", j=NCH))
+                q_sb[b] = t1
 
-        for kind, b in (("k", 0), ("q", 0), ("v", 0), ("v", 1), ("k", 1), ("q", 1)):
-            load(kind, b)
-        for b in range(2, B):
-            load("k", b)
-            load("q", b)
+        load("k", 0)
+        load("q", 0)
+        for b in range(0, B, 2):
             load("v", b)
+            for bb in (b + 1, b + 2):
+                if bb < B:
+                    load("k", bb)
+                    load("q", bb)
 
         idz = const.tile([P, S], F32, name="idz")
         nc.gpsimd.memset(idz[:], 0.0)
@@ -69,8 +79,7 @@ def tile_retention_pa_kernel(tc, q_rot, k_rot, v, gamma, out):
             initial=0.0, op0=MULT, op1=ADD,
         )
         dec = const.tile([P, P, NCH], F32, name="dec")
-        for s in range(NCH):
-            nc.vector.tensor_copy(out=dec[:, :, s], in_=w[:, (NCH - 1 - s) * P : (NCH - s) * P])
+        nc.vector.tensor_copy(out=dec[:], in_=w[:].rearrange("p (s r) -> p r s", s=NCH))
 
         qT, kT, scs, s01s, vgs, vcs, vss, pcs, pss = {}, {}, {}, {}, {}, {}, {}, {}, {}
 
@@ -101,17 +110,17 @@ def tile_retention_pa_kernel(tc, q_rot, k_rot, v, gamma, out):
             if not ok(b):
                 return
             sc = psum.tile([P, c + 1, P], F32, name="sc%d" % c)
-            for j in range(c + 1):
-                score_tile(b, sc[:, j, :], j, c)
+            for s in range(c + 1):
+                score_tile(b, sc[:, s, :], c - s, c)
             scs[(b, c)] = sc
 
         def decay(b, c):
             if not ok(b):
                 return
             nc.vector.tensor_tensor(
-                out=grouped[b % NG][:, c, :, 0 : c + 1],
-                in0=scs[(b, c)][:].rearrange("p j r -> p r j"),
-                in1=dec[:, :, NCH - 1 - c : NCH],
+                out=grouped[b % NG][:, c, :, NCH - 1 - c : NCH],
+                in0=scs[(b, c)][:].rearrange("p s r -> p r s"),
+                in1=dec[:, :, 0 : c + 1],
                 op=MULT,
             )
 
@@ -120,8 +129,8 @@ def tile_retention_pa_kernel(tc, q_rot, k_rot, v, gamma, out):
                 return
             sc = psum.tile([P, 3, P], F32, name="sc01")
             score_tile(b, sc[:, 0, :], 0, 0)
-            score_tile(b, sc[:, 1, :], 0, 1)
-            score_tile(b, sc[:, 2, :], 1, 1)
+            score_tile(b, sc[:, 1, :], 1, 1)
+            score_tile(b, sc[:, 2, :], 0, 1)
             s01 = work2.tile([P, 3, P], F32, name="s01")
             nc.scalar.copy(out=s01[:], in_=sc[:])
             s01s[b] = s01
@@ -130,11 +139,11 @@ def tile_retention_pa_kernel(tc, q_rot, k_rot, v, gamma, out):
             if not ok(b):
                 return
             g = grouped[b % NG]
-            nc.gpsimd.tensor_tensor(out=g[:, 0, :, 0], in0=s01s[b][:, 0, :], in1=w[:, 0:P], op=MULT)
+            nc.gpsimd.tensor_tensor(out=g[:, 0, :, NCH - 1], in0=s01s[b][:, 0, :], in1=w[:, 0:P], op=MULT)
             nc.gpsimd.tensor_tensor(
-                out=g[:, 1, :, 0:2],
-                in0=s01s[b][:, 1:3, :].rearrange("p j r -> p r j"),
-                in1=dec[:, :, 2:4],
+                out=g[:, 1, :, NCH - 2 : NCH],
+                in0=s01s[b][:, 1:3, :].rearrange("p s r -> p r s"),
+                in1=dec[:, :, 0:2],
                 op=MULT,
             )
 
@@ -144,7 +153,7 @@ def tile_retention_pa_kernel(tc, q_rot, k_rot, v, gamma, out):
             vg = work3.tile([P, D, NCH], BF16, name="vg", align_bytes=64)
             nc.vector.tensor_copy(
                 out=vg[:].rearrange("p (c i) t -> p c t i", i=4),
-                in_=v_sb[b][:].rearrange("p t (c i) -> p c t i", i=4),
+                in_=v_sb[b].rearrange("p t (c i) -> p c t i", i=4),
             )
             vgs[b] = vg
 
@@ -191,10 +200,17 @@ def tile_retention_pa_kernel(tc, q_rot, k_rot, v, gamma, out):
 
         transpose(0, "k")
         transpose(0, "q")
+        regroup_v(0)
+        quantise_v(0)
+        scores(0, 2)
         scores01(0)
         decay01(0)
-        regroup_v(0)
-        for k in range(-1, B):
+        scores(0, 3)
+        transpose(1, "k")
+        transpose(1, "q")
+        scores01(1)
+        decay01(1)
+        for k in range(B):
             last = k == B - 1
             if ok(k - 1):
                 second_matmul_half(k - 1, 0)
@@ -205,6 +221,8 @@ def tile_retention_pa_kernel(tc, q_rot, k_rot, v, gamma, out):
             elif k > 0:
                 transpose(k + 3, "k")
             decay(k, 2)
+            if k == 0:
+                regroup_v(1)
             if last:
                 quantise_p(k, 0, 2)
             scores(k + 1, 2)
@@ -215,9 +233,6 @@ def tile_retention_pa_kernel(tc, q_rot, k_rot, v, gamma, out):
                 transpose(k + 3, "q")
             decay(k, 3)
             scores(k + 1, 3)
-            if k == -1:
-                transpose(1, "k")
-                transpose(1, "q")
             scores01(k + 2)
             regroup_v(k + 2)
             quantise_v(k + 1)

@@ -24,7 +24,6 @@ def tile_retention_pa_kernel(tc, q_rot, k_rot, v, gamma, out):
         const = ctx.enter_context(tc.tile_pool(name="const", bufs=1))
         inp = ctx.enter_context(tc.tile_pool(name="inp", bufs=1))
         work2 = ctx.enter_context(tc.tile_pool(name="work2", bufs=2))
-        work3 = ctx.enter_context(tc.tile_pool(name="work3", bufs=3))
         work4 = ctx.enter_context(tc.tile_pool(name="work4", bufs=4))
         psum = ctx.enter_context(tc.psum_pool(name="psum", bufs=1))
         ctx.enter_context(tc.manual_schedule())
@@ -66,11 +65,16 @@ def tile_retention_pa_kernel(tc, q_rot, k_rot, v, gamma, out):
         nc.gpsimd.memset(idz[:], 0.0)
         make_identity(nc, idz[:, 0:P])
         ident = idz[:, 0:P]
-        grouped = []
-        for i in range(NG):
-            g = const.tile([P, NCH, P, NCH], BF16, name="grouped%d" % i, align_bytes=64)
-            nc.vector.memset(g[:], 0.0)
-            grouped.append(g)
+        GW = NCH * P * NCH
+        VW = D * NCH
+        even = const.tile([P, GW], BF16, name="even", align_bytes=64)
+        odd = const.tile([P, GW + 2 * VW], BF16, name="odd", align_bytes=64)
+        first_v = const.tile([P, 2 * VW], BF16, name="first_v", align_bytes=64)
+        nc.vector.memset(even[:], 0.0)
+        nc.vector.memset(odd[:, 0:GW], 0.0)
+        grouped = [
+            t[:, 0:GW].rearrange("p (c r j) -> p c r j", c=NCH, r=P) for t in (even, odd)
+        ]
         gam = const.tile([P, 1], F32, name="gam")
         nc.vector.tensor_copy(out=gam[:], in_=gam_bf[:])
         w = const.tile([P, S], F32, name="w")
@@ -81,7 +85,7 @@ def tile_retention_pa_kernel(tc, q_rot, k_rot, v, gamma, out):
         dec = const.tile([P, P, NCH], F32, name="dec")
         nc.vector.tensor_copy(out=dec[:], in_=w[:].rearrange("p (s r) -> p r s", s=NCH))
 
-        qT, kT, scs, s01s, vgs, vcs, vss, pcs, pss = {}, {}, {}, {}, {}, {}, {}, {}, {}
+        qT, kT, scs, s01s, vcs, vss, pcs, pss = {}, {}, {}, {}, {}, {}, {}, {}
 
         def ok(b):
             return 0 <= b < B
@@ -150,31 +154,37 @@ def tile_retention_pa_kernel(tc, q_rot, k_rot, v, gamma, out):
         def regroup_v(b):
             if not ok(b):
                 return
-            vg = work3.tile([P, D, NCH], BF16, name="vg", align_bytes=64)
+            if b < 2:
+                vg = first_v[:, b * VW : (b + 1) * VW]
+            else:
+                vg = odd[:, GW + (b % 2) * VW : GW + (b % 2 + 1) * VW]
             nc.vector.tensor_copy(
-                out=vg[:].rearrange("p (c i) t -> p c t i", i=4),
+                out=vg.rearrange("p (c i t) -> p c t i", i=4, t=NCH),
                 in_=v_sb[b].rearrange("p t (c i) -> p c t i", i=4),
             )
-            vgs[b] = vg
 
-        def quantise_v(b):
-            if not ok(b):
-                return
-            vc = work3.tile([P, D], U32, name="vc", align_bytes=64)
-            vs = work3.tile([P, D], U8, name="vs", align_bytes=64)
-            nc.vector.quantize_mx(
-                out=vc[:].bitcast(FP8X4), scales=vs[:],
-                in_=vgs[b][:].rearrange("p d t -> p (d t)"),
-            )
-            vcs[b], vss[b] = vc, vs
+        def quantise_first_v():
+            vc = const.tile([P, 2 * D], U32, name="vc01", align_bytes=64)
+            vs = const.tile([P, 2 * D], U8, name="vs01", align_bytes=64)
+            nc.vector.quantize_mx(out=vc[:].bitcast(FP8X4), scales=vs[:], in_=first_v[:])
+            for b in range(2):
+                vcs[b], vss[b] = vc[:, b * D : (b + 1) * D], vs[:, b * D : (b + 1) * D]
 
-        def quantise_p(b, c0, c1):
+        def quantise_p(b, c0, c1, with_v):
+            width = S + 2 * D if b % 2 else S
             if c0 == 0:
-                pcs[b] = work3.tile([P, S], U32, name="pc", align_bytes=64)
-                pss[b] = work3.tile([P, S], U8, name="ps", align_bytes=64)
+                pcs[b] = work2.tile([P, width], U32, name="pc%d" % (b % 2), align_bytes=64)
+                pss[b] = work2.tile([P, width], U8, name="ps%d" % (b % 2), align_bytes=64)
+            src = odd if b % 2 else even
+            lo, hi = c0 * P, c1 * P
+            if with_v:
+                hi = width
+                for i in range(2):
+                    vcs[b + 1 + i] = pcs[b][:, S + i * D : S + (i + 1) * D]
+                    vss[b + 1 + i] = pss[b][:, S + i * D : S + (i + 1) * D]
             nc.vector.quantize_mx(
-                out=pcs[b][:, c0 * P : c1 * P].bitcast(FP8X4), scales=pss[b][:, c0 * P : c1 * P],
-                in_=grouped[b % NG][:, c0:c1].rearrange("p c r j -> p (c r j)"),
+                out=pcs[b][:, lo:hi].bitcast(FP8X4), scales=pss[b][:, lo:hi],
+                in_=src[:, NCH * lo : NCH * hi],
             )
 
         def mx_pass(b, c, dst):
@@ -182,8 +192,8 @@ def tile_retention_pa_kernel(tc, q_rot, k_rot, v, gamma, out):
                 dst,
                 lhsT=pcs[b][:, c * P : (c + 1) * P].bitcast(FP8X4),
                 lhsT_scale=pss[b][:, c * P : (c + 1) * P],
-                rhs=vcs[b][:].bitcast(FP8X4),
-                rhs_scale=vss[b][:],
+                rhs=vcs[b].bitcast(FP8X4),
+                rhs_scale=vss[b],
                 start=True, stop=True,
             )
 
@@ -201,7 +211,7 @@ def tile_retention_pa_kernel(tc, q_rot, k_rot, v, gamma, out):
         transpose(0, "k")
         transpose(0, "q")
         regroup_v(0)
-        quantise_v(0)
+        regroup_v(1)
         scores(0, 2)
         scores01(0)
         decay01(0)
@@ -210,37 +220,33 @@ def tile_retention_pa_kernel(tc, q_rot, k_rot, v, gamma, out):
         transpose(1, "q")
         scores01(1)
         decay01(1)
+        transpose(2, "k")
+        transpose(2, "q")
         for k in range(B):
             last = k == B - 1
             if ok(k - 1):
                 second_matmul_half(k - 1, 0)
                 second_matmul_half(k - 1, 1)
-            if k == 0:
-                transpose(2, "k")
-                transpose(2, "q")
-            elif k > 0:
-                transpose(k + 3, "k")
             decay(k, 2)
-            if k == 0:
-                regroup_v(1)
             if last:
-                quantise_p(k, 0, 2)
+                quantise_p(k, 0, 2, False)
             scores(k + 1, 2)
-            if k == 0:
-                transpose(3, "k")
-                transpose(3, "q")
-            elif k > 0:
-                transpose(k + 3, "q")
             decay(k, 3)
             scores(k + 1, 3)
             scores01(k + 2)
-            regroup_v(k + 2)
-            quantise_v(k + 1)
-            if last:
-                second_matmul_half(k, 0)
-                quantise_p(k, 2, 4)
-            elif ok(k):
-                quantise_p(k, 0, 4)
+            transpose(k + 3, "k")
+            transpose(k + 3, "q")
+            if k == 0:
+                quantise_first_v()
+                quantise_p(k, 0, 4, False)
+                regroup_v(2)
+            else:
+                regroup_v(k + 2)
+                if last:
+                    second_matmul_half(k, 0)
+                    quantise_p(k, 2, 4, False)
+                else:
+                    quantise_p(k, 0, 4, k % 2 == 1)
             decay01(k + 2)
 
         b = B - 1

@@ -52,9 +52,9 @@ def tile_retention_pa_kernel(tc, q_rot, k_rot, v, gamma, out):
                 nc.sync.dma_start(out=t1[:], in_=q_rot[b].rearrange("(p j) d -> p j d", j=NCH))
                 q_sb[b] = t1
 
-        load("k", 0)
-        load("q", 0)
-        for b in range(0, B, 2):
+        for kind, b in (("k", 0), ("q", 0), ("k", 1), ("q", 1), ("v", 0), ("k", 2), ("q", 2)):
+            load(kind, b)
+        for b in range(2, B, 2):
             load("v", b)
             for bb in (b + 1, b + 2):
                 if bb < B:
@@ -210,18 +210,18 @@ def tile_retention_pa_kernel(tc, q_rot, k_rot, v, gamma, out):
 
         transpose(0, "k")
         transpose(0, "q")
-        regroup_v(0)
-        regroup_v(1)
+        transpose(1, "k")
+        transpose(1, "q")
         scores(0, 2)
         scores01(0)
         decay01(0)
         scores(0, 3)
-        transpose(1, "k")
-        transpose(1, "q")
-        scores01(1)
-        decay01(1)
         transpose(2, "k")
         transpose(2, "q")
+        regroup_v(0)
+        regroup_v(1)
+        scores01(1)
+        decay01(1)
         for k in range(B):
             last = k == B - 1
             if ok(k - 1):
@@ -233,9 +233,9 @@ def tile_retention_pa_kernel(tc, q_rot, k_rot, v, gamma, out):
             scores(k + 1, 2)
             decay(k, 3)
             scores(k + 1, 3)
-            scores01(k + 2)
             transpose(k + 3, "k")
             transpose(k + 3, "q")
+            scores01(k + 2)
             if k == 0:
                 quantise_first_v()
                 quantise_p(k, 0, 4, False)

@@ -25,6 +25,7 @@ def tile_retention_pa_kernel(tc, q_rot, k_rot, v, gamma, out):
         inp = ctx.enter_context(tc.tile_pool(name="inp", bufs=1))
         work2 = ctx.enter_context(tc.tile_pool(name="work2", bufs=2))
         work4 = ctx.enter_context(tc.tile_pool(name="work4", bufs=4))
+        outp = ctx.enter_context(tc.tile_pool(name="outp", bufs=2 * B))
         psum = ctx.enter_context(tc.psum_pool(name="psum", bufs=1))
         ctx.enter_context(tc.manual_schedule())
 
@@ -52,9 +53,9 @@ def tile_retention_pa_kernel(tc, q_rot, k_rot, v, gamma, out):
                 nc.sync.dma_start(out=t1[:], in_=q_rot[b].rearrange("(p j) d -> p j d", j=NCH))
                 q_sb[b] = t1
 
-        for kind, b in (("k", 0), ("q", 0), ("k", 1), ("q", 1), ("v", 0), ("k", 2), ("q", 2)):
-            load(kind, b)
-        for b in range(2, B, 2):
+        load("k", 0)
+        load("q", 0)
+        for b in range(0, B, 2):
             load("v", b)
             for bb in (b + 1, b + 2):
                 if bb < B:
@@ -201,7 +202,7 @@ def tile_retention_pa_kernel(tc, q_rot, k_rot, v, gamma, out):
             o = psum.tile([P, 2, D], F32, name="o%d" % h)
             for i in range(2):
                 mx_pass(b, 2 * h + i, o[:, i, :])
-            ot = work4.tile([P, 2, D], F32, name="ot")
+            ot = outp.tile([P, 2, D], F32, name="ot")
             nc.scalar.copy(out=ot[:], in_=o[:])
             nc.sync.dma_start(
                 out=out[b, 2 * h * P : (2 * h + 2) * P, :].rearrange("(c r) d -> r c d", r=P),
@@ -210,18 +211,18 @@ def tile_retention_pa_kernel(tc, q_rot, k_rot, v, gamma, out):
 
         transpose(0, "k")
         transpose(0, "q")
-        transpose(1, "k")
-        transpose(1, "q")
+        regroup_v(0)
+        regroup_v(1)
         scores(0, 2)
         scores01(0)
         decay01(0)
         scores(0, 3)
-        transpose(2, "k")
-        transpose(2, "q")
-        regroup_v(0)
-        regroup_v(1)
+        transpose(1, "k")
+        transpose(1, "q")
         scores01(1)
         decay01(1)
+        transpose(2, "k")
+        transpose(2, "q")
         for k in range(B):
             last = k == B - 1
             if ok(k - 1):
@@ -233,9 +234,9 @@ def tile_retention_pa_kernel(tc, q_rot, k_rot, v, gamma, out):
             scores(k + 1, 2)
             decay(k, 3)
             scores(k + 1, 3)
+            scores01(k + 2)
             transpose(k + 3, "k")
             transpose(k + 3, "q")
-            scores01(k + 2)
             if k == 0:
                 quantise_first_v()
                 quantise_p(k, 0, 4, False)
@@ -256,7 +257,7 @@ def tile_retention_pa_kernel(tc, q_rot, k_rot, v, gamma, out):
         mx_pass(b, 3, o_b[:])
         ot_a = work4.tile([P, D], F32, name="ot_a")
         nc.scalar.copy(out=ot_a[:], in_=o_a[:])
-        nc.scalar.dma_start(out=out[b, 2 * P : 3 * P, :], in_=ot_a[:])
+        nc.sync.dma_start(out=out[b, 2 * P : 3 * P, :], in_=ot_a[:])
         ot_b = work4.tile([P, D], F32, name="ot_b")
         nc.vector.tensor_copy(out=ot_b[:], in_=o_b[:])
         nc.sync.dma_start(out=out[b, 3 * P : 4 * P, :], in_=ot_b[:])

@@ -53,9 +53,9 @@ def tile_retention_pa_kernel(tc, q_rot, k_rot, v, gamma, out):
                 nc.sync.dma_start(out=t1[:], in_=q_rot[b].rearrange("(p j) d -> p j d", j=NCH))
                 q_sb[b] = t1
 
-        load("k", 0)
-        load("q", 0)
-        for b in range(0, B, 2):
+        for kind, b in (("k", 0), ("q", 0), ("k", 1), ("q", 1), ("v", 0), ("k", 2), ("q", 2)):
+            load(kind, b)
+        for b in range(2, B, 2):
             load("v", b)
             for bb in (b + 1, b + 2):
                 if bb < B:
@@ -211,28 +211,30 @@ def tile_retention_pa_kernel(tc, q_rot, k_rot, v, gamma, out):
 
         transpose(0, "k")
         transpose(0, "q")
-        regroup_v(0)
-        regroup_v(1)
+        transpose(1, "k")
+        transpose(1, "q")
         scores(0, 2)
         scores01(0)
         decay01(0)
         scores(0, 3)
-        transpose(1, "k")
-        transpose(1, "q")
-        scores01(1)
-        decay01(1)
         transpose(2, "k")
         transpose(2, "q")
+        scores01(1)
+        decay01(1)
         for k in range(B):
             last = k == B - 1
             if ok(k - 1):
                 second_matmul_half(k - 1, 0)
                 second_matmul_half(k - 1, 1)
             decay(k, 2)
+            if k == 0:
+                regroup_v(0)
             if last:
                 quantise_p(k, 0, 2, False)
             scores(k + 1, 2)
             decay(k, 3)
+            if k == 0:
+                regroup_v(1)
             scores(k + 1, 3)
             scores01(k + 2)
             transpose(k + 3, "k")

from contextlib import ExitStack

import concourse.mybir as mybir
from concourse.masks import make_identity

F32 = mybir.dt.float32
BF16 = mybir.dt.bfloat16
U32 = mybir.dt.uint32
U8 = mybir.dt.uint8
FP8X4 = mybir.dt.float8_e4m3fn_x4
MULT = mybir.AluOpType.mult
ADD = mybir.AluOpType.add

B, S, D = 8, 512, 256
P = 128
NCH = S // P
FLOPS = 4 * B * S * S * D
NG = 2


def tile_retention_pa_kernel(tc, q_rot, k_rot, v, gamma, out):
    nc = tc.nc
    with ExitStack() as ctx:
        const = ctx.enter_context(tc.tile_pool(name="const", bufs=1))
        inp = ctx.enter_context(tc.tile_pool(name="inp", bufs=1))
        work2 = ctx.enter_context(tc.tile_pool(name="work2", bufs=2))
        work4 = ctx.enter_context(tc.tile_pool(name="work4", bufs=4))
        outp = ctx.enter_context(tc.tile_pool(name="outp", bufs=2 * B))
        psum = ctx.enter_context(tc.psum_pool(name="psum", bufs=1))
        ctx.enter_context(tc.manual_schedule())

        gam_bf = const.tile([P, 1], BF16, name="gam_bf")
        nc.scalar.dma_start(out=gam_bf[:], in_=gamma.partition_broadcast(P))
        q_sb, k_sb, v_sb = {}, {}, {}

        def load(kind, b):
            if kind == "v":
                t2 = inp.tile([P, 2, NCH, D], BF16, name="v_sb%d" % b)
                for t in range(NCH):
                    j = NCH - 1 - t
                    nc.sync.dma_start(
                        out=t2[:, :, t, :],
                        in_=v[b : b + 2, j * P : (j + 1) * P, :].rearrange("b p d -> p b d"),
                    )
                v_sb[b] = t2[:, 0]
                v_sb[b + 1] = t2[:, 1]
                return
            t1 = inp.tile([P, NCH, D], BF16, name="%s_sb%d" % (kind, b))
            if kind == "k":
                nc.sync.dma_start(out=t1[:], in_=k_rot[b].rearrange("(p j) d -> p j d", j=NCH))
                k_sb[b] = t1
            else:
                nc.sync.dma_start(out=t1[:], in_=q_rot[b].rearrange("(p j) d -> p j d", j=NCH))
                q_sb[b] = t1

        for kind, b in (("k", 0), ("q", 0), ("k", 1), ("q", 1), ("v", 0), ("k", 2), ("q", 2)):
            load(kind, b)
        for b in range(2, B, 2):
            load("v", b)
            for bb in (b + 1, b + 2):
                if bb < B:
                    load("k", bb)
                    load("q", bb)

        idz = const.tile([P, S], F32, name="idz")
        nc.gpsimd.memset(idz[:], 0.0)
        make_identity(nc, idz[:, 0:P])
        ident = idz[:, 0:P]
        GW = NCH * P * NCH
        VW = D * NCH
        even = const.tile([P, GW], BF16, name="even", align_bytes=64)
        odd = const.tile([P, GW + 2 * VW], BF16, name="odd", align_bytes=64)
        first_v = const.tile([P, 2 * VW], BF16, name="first_v", align_bytes=64)
        nc.vector.memset(even[:], 0.0)
        nc.vector.memset(odd[:, 0:GW], 0.0)
        grouped = [
            t[:, 0:GW].rearrange("p (c r j) -> p c r j", c=NCH, r=P) for t in (even, odd)
        ]
        gam = const.tile([P, 1], F32, name="gam")
        nc.vector.tensor_copy(out=gam[:], in_=gam_bf[:])
        w = const.tile([P, S], F32, name="w")
        nc.vector.tensor_tensor_scan(
            out=w[:], data0=gam[:, 0:1].to_broadcast([P, S]), data1=idz[:],
            initial=0.0, op0=MULT, op1=ADD,
        )
        dec = const.tile([P, P, NCH], F32, name="dec")
        nc.vector.tensor_copy(out=dec[:], in_=w[:].rearrange("p (s r) -> p r s", s=NCH))

        qT, kT, scs, s01s, vcs, vss, pcs, pss = {}, {}, {}, {}, {}, {}, {}, {}

        def ok(b):
            return 0 <= b < B

        def transpose(b, kind):
            if not ok(b):
                return
            src, dst = (k_sb, kT) if kind == "k" else (q_sb, qT)
            tp = psum.tile([P, NCH, P], F32, name="tp_" + kind)
            for j in range(NCH):
                nc.tensor.transpose(tp[:, j, :], src[b][:, j, :].bitcast(F32), ident)
            t = work4.tile([P, P, NCH], F32, name=kind + "T")
            nc.scalar.copy(out=t[:], in_=tp[:].rearrange("w j p -> w p j"))
            dst[b] = t[:].rearrange("w p j -> w (p j)").bitcast(BF16).rearrange("w (n e) -> w n e", e=2)

        def score_tile(b, dst, j, c):
            for e in range(2):
                nc.tensor.matmul(
                    dst,
                    lhsT=kT[b][:, j * P : (j + 1) * P, e],
                    rhs=qT[b][:, c * P : (c + 1) * P, e],
                    start=(e == 0), stop=(e == 1),
                )

        def scores(b, c):
            if not ok(b):
                return
            sc = psum.tile([P, c + 1, P], F32, name="sc%d" % c)
            for s in range(c + 1):
                score_tile(b, sc[:, s, :], c - s, c)
            scs[(b, c)] = sc

        def decay(b, c):
            if not ok(b):
                return
            nc.vector.tensor_tensor(
                out=grouped[b % NG][:, c, :, NCH - 1 - c : NCH],
                in0=scs[(b, c)][:].rearrange("p s r -> p r s"),
                in1=dec[:, :, 0 : c + 1],
                op=MULT,
            )

        def scores01(b):
            if not ok(b):
                return
            sc = psum.tile([P, 3, P], F32, name="sc01")
            score_tile(b, sc[:, 0, :], 0, 0)
            score_tile(b, sc[:, 1, :], 1, 1)
            score_tile(b, sc[:, 2, :], 0, 1)
            s01 = work2.tile([P, 3, P], F32, name="s01")
            nc.scalar.copy(out=s01[:], in_=sc[:])
            s01s[b] = s01

        def decay01(b):
            if not ok(b):
                return
            g = grouped[b % NG]
            nc.gpsimd.tensor_tensor(out=g[:, 0, :, NCH - 1], in0=s01s[b][:, 0, :], in1=w[:, 0:P], op=MULT)
            nc.gpsimd.tensor_tensor(
                out=g[:, 1, :, NCH - 2 : NCH],
                in0=s01s[b][:, 1:3, :].rearrange("p s r -> p r s"),
                in1=dec[:, :, 0:2],
                op=MULT,
            )

        def regroup_v(b):
            if not ok(b):
                return
            if b < 2:
                vg = first_v[:, b * VW : (b + 1) * VW]
            else:
                vg = odd[:, GW + (b % 2) * VW : GW + (b % 2 + 1) * VW]
            nc.vector.tensor_copy(
                out=vg.rearrange("p (c i t) -> p c t i", i=4, t=NCH),
                in_=v_sb[b].rearrange("p t (c i) -> p c t i", i=4),
            )

        def quantise_first_v():
            vc = const.tile([P, 2 * D], U32, name="vc01", align_bytes=64)
            vs = const.tile([P, 2 * D], U8, name="vs01", align_bytes=64)
            nc.vector.quantize_mx(out=vc[:].bitcast(FP8X4), scales=vs[:], in_=first_v[:])
            for b in range(2):
                vcs[b], vss[b] = vc[:, b * D : (b + 1) * D], vs[:, b * D : (b + 1) * D]

        def quantise_p(b, c0, c1, with_v):
            width = S + 2 * D if b % 2 else S
            if c0 == 0:
                pcs[b] = work2.tile([P, width], U32, name="pc%d" % (b % 2), align_bytes=64)
                pss[b] = work2.tile([P, width], U8, name="ps%d" % (b % 2), align_bytes=64)
            src = odd if b % 2 else even
            lo, hi = c0 * P, c1 * P
            if with_v:
                hi = width
                for i in range(2):
                    vcs[b + 1 + i] = pcs[b][:, S + i * D : S + (i + 1) * D]
                    vss[b + 1 + i] = pss[b][:, S + i * D : S + (i + 1) * D]
            nc.vector.quantize_mx(
                out=pcs[b][:, lo:hi].bitcast(FP8X4), scales=pss[b][:, lo:hi],
                in_=src[:, NCH * lo : NCH * hi],
            )

        def mx_pass(b, c, dst):
            nc.tensor.matmul_mx(
                dst,
                lhsT=pcs[b][:, c * P : (c + 1) * P].bitcast(FP8X4),
                lhsT_scale=pss[b][:, c * P : (c + 1) * P],
                rhs=vcs[b].bitcast(FP8X4),
                rhs_scale=vss[b],
                start=True, stop=True,
            )

        def second_matmul_half(b, h):
            o = psum.tile([P, 2, D], F32, name="o%d" % h)
            for i in range(2):
                mx_pass(b, 2 * h + i, o[:, i, :])
            ot = outp.tile([P, 2, D], F32, name="ot")
            nc.scalar.copy(out=ot[:], in_=o[:])
            nc.sync.dma_start(
                out=out[b, 2 * h * P : (2 * h + 2) * P, :].rearrange("(c r) d -> r c d", r=P),
                in_=ot[:],
            )

        transpose(0, "k")
        transpose(0, "q")
        transpose(1, "k")
        transpose(1, "q")
        scores(0, 2)
        scores01(0)
        decay01(0)
        scores(0, 3)
        transpose(2, "k")
        transpose(2, "q")
        scores01(1)
        decay01(1)
        for k in range(B):
            last = k == B - 1
            if ok(k - 1):
                second_matmul_half(k - 1, 0)
                second_matmul_half(k - 1, 1)
            decay(k, 2)
            if k == 0:
                regroup_v(0)
            if last:
                quantise_p(k, 0, 2, False)
            scores(k + 1, 2)
            decay(k, 3)
            if k == 0:
                regroup_v(1)
            scores(k + 1, 3)
            scores01(k + 2)
            transpose(k + 3, "k")
            transpose(k + 3, "q")
            if k == 0:
                quantise_first_v()
                quantise_p(k, 0, 4, False)
                regroup_v(2)
            else:
                regroup_v(k + 2)
                if last:
                    second_matmul_half(k, 0)
                    quantise_p(k, 2, 4, False)
                else:
                    quantise_p(k, 0, 4, k % 2 == 1)
            decay01(k + 2)

        b = B - 1
        o_a = psum.tile([P, D], F32, name="o1")
        mx_pass(b, 2, o_a[:])
        o_b = psum.tile([P, D], F32, name="o2")
        mx_pass(b, 3, o_b[:])
        ot_a = work4.tile([P, D], F32, name="ot_a")
        nc.scalar.copy(out=ot_a[:], in_=o_a[:])
        nc.sync.dma_start(out=out[b, 2 * P : 3 * P, :], in_=ot_a[:])
        ot_b = work4.tile([P, D], F32, name="ot_b")
        nc.vector.tensor_copy(out=ot_b[:], in_=o_b[:])
        nc.sync.dma_start(out=out[b, 3 * P : 4 * P, :], in_=ot_b[:])
